import numpy as np
import ml_dtypes

BF16 = ml_dtypes.bfloat16


def bf(x):
    return np.asarray(x, np.float32).astype(BF16)


def f32(x):
    return np.asarray(x, np.float32)


def f64(x):
    return np.asarray(x).astype(np.float64)


def striped(idx):
    return np.tile(idx.reshape(-1, 16).T, (8, 1))


F, C, S, K, T, H, N = 4096, 128, 1024, 4, 2, 512, 8192


def setup_inputs():
    return {"z": bf(np.random.standard_normal((F, S))), "wsv": bf(np.random.standard_normal((F, C)) / np.sqrt(F)), "wsr": bf(np.random.standard_normal((F, C)) / np.sqrt(F)), "wdr": bf(np.random.standard_normal((F, C)) / np.sqrt(F)), "offs": striped(np.concatenate([np.random.permutation(S)[:H] for _ in range(N // H)]))}


def reference(z, wsv, wsr, wdr, offs):
    idx = offs[:16].T.reshape(-1)
    nb = idx.reshape(T, K, S)
    zz = f64(z)
    node = f64(wsv).T @ zz
    ps = f64(wsr).T @ zz
    pd = f64(wdr).T @ zz
    agg_s = ps[:, nb[0]].sum(axis=1) / K
    agg_d = pd[:, nb[1]].sum(axis=1) / K
    return np.maximum(node + agg_s + agg_d, 0.0)

@@ -1,0 +1,78 @@
+import concourse.mybir as mybir
+from concourse.masks import make_identity
+
+BF16, F32, U16 = mybir.dt.bfloat16, mybir.dt.float32, mybir.dt.uint16
+
+P = 128
+F = 4096
+S = 1024
+SLOTS = 4
+N = 2 * SLOTS * S
+PIECE = 512
+HALVES = S // PIECE
+CHUNKS = F // P
+GROUP = 4
+
+FLOPS = 3 * 2 * F * P * S
+
+
+def tile_gnn_layer_b_kernel(tc, z, wsv, wsr, wdr, offs, out):
+    nc = tc.nc
+    z_rows = z.rearrange("(p a) s -> p a s", p=P)
+    w_rows = [w.rearrange("(p a) c -> p a c", p=P) for w in (wsr, wdr, wsv)]
+
+    with (
+        tc.tile_pool(name="held", bufs=1) as held,
+        tc.psum_pool(name="psum", bufs=1) as psum,
+    ):
+        offsets = held.tile([P, N // 16], U16, name="offsets")
+        nc.sync.dma_start(offsets[:], offs)
+
+        z_groups, w_groups = [], []
+        for g in range(CHUNKS // GROUP):
+            chunks = slice(g * GROUP, (g + 1) * GROUP)
+            z_group = held.tile([P, GROUP, S], BF16, name=f"z{g}")
+            nc.sync.dma_start(z_group[:], z_rows[:, chunks, :])
+            z_groups.append(z_group)
+            w_group = [held.tile([P, GROUP, P], BF16, name=f"w{m}_{g}") for m in range(3)]
+            for m in range(3):
+                nc.scalar.dma_start(w_group[m][:], w_rows[m][:, chunks, :])
+            w_groups.append(w_group)
+
+        identity = held.tile([P, P], BF16, name="identity")
+        make_identity(nc, identity[:])
+        quarter = held.tile([P, P], BF16, name="quarter")
+        nc.vector.tensor_scalar_mul(quarter[:], identity[:], 1.0 / SLOTS)
+
+        sums = [[psum.tile([P, PIECE], F32, name=f"sum{m}_{h}") for h in range(HALVES)] for m in range(3)]
+        for a in range(CHUNKS):
+            g, i = divmod(a, GROUP)
+            for m in range(3):
+                for h in range(HALVES):
+                    nc.tensor.matmul(
+                        sums[m][h][:],
+                        w_groups[g][m][:, i, :],
+                        z_groups[g][:, i, h * PIECE : (h + 1) * PIECE],
+                        start=(a == 0),
+                        stop=(a == CHUNKS - 1 and m < 2),
+                    )
+
+        tables = [held.tile([P, S], BF16, name=f"table{m}") for m in range(2)]
+        for m in range(2):
+            nc.vector.tensor_copy(tables[m][:, 0:PIECE], sums[m][0][:])
+            nc.scalar.copy(tables[m][:, PIECE:S], sums[m][1][:])
+
+        for h in range(HALVES):
+            for m in range(2):
+                for k in range(SLOTS):
+                    first = (m * SLOTS * S + k * S + h * PIECE) // 16
+                    nc.tensor.matmul(
+                        sums[2][h][:],
+                        quarter[:],
+                        tables[m][:].indirect(offsets[:, first : first + PIECE // 16]),
+                        start=False,
+                        stop=(m == 1 and k == SLOTS - 1),
+                    )
+            result = held.tile([P, PIECE], F32, name=f"result{h}")
+            nc.vector.tensor_relu(result[:], sums[2][h][:])
+            nc.sync.dma_start(out[:, h * PIECE : (h + 1) * PIECE], result[:])

@@ -11,7 +11,8 @@ N = 2 * SLOTS * S
 PIECE = 512
 HALVES = S // PIECE
 CHUNKS = F // P
-GROUP = 4
+LOADS = (1, 1) + (2,) * 15
+assert sum(LOADS) == CHUNKS
 
 FLOPS = 3 * 2 * F * P * S
 
@@ -25,19 +26,19 @@ def tile_gnn_layer_b_kernel(tc, z, wsv, wsr, wdr, offs, out):
         tc.tile_pool(name="held", bufs=1) as held,
         tc.psum_pool(name="psum", bufs=1) as psum,
     ):
+        z_chunks, w_chunks = [], [[], [], []]
+        for g, size in enumerate(LOADS):
+            chunks = slice(len(z_chunks), len(z_chunks) + size)
+            z_load = held.tile([P, size, S], BF16, name=f"z{g}")
+            nc.sync.dma_start(z_load[:], z_rows[:, chunks, :])
+            z_chunks.extend(z_load[:, i, :] for i in range(size))
+            for m in range(3):
+                w_load = held.tile([P, size, P], BF16, name=f"w{m}_{g}")
+                nc.scalar.dma_start(w_load[:], w_rows[m][:, chunks, :])
+                w_chunks[m].extend(w_load[:, i, :] for i in range(size))
+
         offsets = held.tile([P, N // 16], U16, name="offsets")
         nc.sync.dma_start(offsets[:], offs)
-
-        z_groups, w_groups = [], []
-        for g in range(CHUNKS // GROUP):
-            chunks = slice(g * GROUP, (g + 1) * GROUP)
-            z_group = held.tile([P, GROUP, S], BF16, name=f"z{g}")
-            nc.sync.dma_start(z_group[:], z_rows[:, chunks, :])
-            z_groups.append(z_group)
-            w_group = [held.tile([P, GROUP, P], BF16, name=f"w{m}_{g}") for m in range(3)]
-            for m in range(3):
-                nc.scalar.dma_start(w_group[m][:], w_rows[m][:, chunks, :])
-            w_groups.append(w_group)
 
         identity = held.tile([P, P], BF16, name="identity")
         make_identity(nc, identity[:])
@@ -46,13 +47,12 @@ def tile_gnn_layer_b_kernel(tc, z, wsv, wsr, wdr, offs, out):
 
         sums = [[psum.tile([P, PIECE], F32, name=f"sum{m}_{h}") for h in range(HALVES)] for m in range(3)]
         for a in range(CHUNKS):
-            g, i = divmod(a, GROUP)
             for m in range(3):
                 for h in range(HALVES):
                     nc.tensor.matmul(
                         sums[m][h][:],
-                        w_groups[g][m][:, i, :],
-                        z_groups[g][:, i, h * PIECE : (h + 1) * PIECE],
+                        w_chunks[m][a],
+                        z_chunks[a][:, h * PIECE : (h + 1) * PIECE],
                         start=(a == 0),
                         stop=(a == CHUNKS - 1 and m < 2),
                     )

@@ -14,6 +14,8 @@ CHUNKS = F // P
 LOADS = (1, 1) + (2,) * 15
 assert sum(LOADS) == CHUNKS
 
+WARMUPS = 3
+
 FLOPS = 3 * 2 * F * P * S
 
 
@@ -26,6 +28,12 @@ def tile_gnn_layer_b_kernel(tc, z, wsv, wsr, wdr, offs, out):
         tc.tile_pool(name="held", bufs=1) as held,
         tc.psum_pool(name="psum", bufs=1) as psum,
     ):
+        zeros = held.tile([P, PIECE], BF16, name="zeros")
+        nc.vector.memset(zeros[:], 0.0)
+        unread = psum.tile([P, PIECE], F32, name="unread")
+        for i in range(WARMUPS):
+            nc.tensor.matmul(unread[:], zeros[:, 0:P], zeros[:], start=True, stop=True)
+
         z_chunks, w_chunks = [], [[], [], []]
         for g, size in enumerate(LOADS):
             chunks = slice(len(z_chunks), len(z_chunks) + size)

@@ -14,7 +14,7 @@ CHUNKS = F // P
 LOADS = (1, 1) + (2,) * 15
 assert sum(LOADS) == CHUNKS
 
-WARMUPS = 3
+LAG = 2
 
 FLOPS = 3 * 2 * F * P * S
 
@@ -28,12 +28,6 @@ def tile_gnn_layer_b_kernel(tc, z, wsv, wsr, wdr, offs, out):
         tc.tile_pool(name="held", bufs=1) as held,
         tc.psum_pool(name="psum", bufs=1) as psum,
     ):
-        zeros = held.tile([P, PIECE], BF16, name="zeros")
-        nc.vector.memset(zeros[:], 0.0)
-        unread = psum.tile([P, PIECE], F32, name="unread")
-        for i in range(WARMUPS):
-            nc.tensor.matmul(unread[:], zeros[:, 0:P], zeros[:], start=True, stop=True)
-
         z_chunks, w_chunks = [], [[], [], []]
         for g, size in enumerate(LOADS):
             chunks = slice(len(z_chunks), len(z_chunks) + size)
@@ -54,21 +48,30 @@ def tile_gnn_layer_b_kernel(tc, z, wsv, wsr, wdr, offs, out):
         nc.vector.tensor_scalar_mul(quarter[:], identity[:], 1.0 / SLOTS)
 
         sums = [[psum.tile([P, PIECE], F32, name=f"sum{m}_{h}") for h in range(HALVES)] for m in range(3)]
+
+        def project(m, a):
+            for h in range(HALVES):
+                nc.tensor.matmul(
+                    sums[m][h][:],
+                    w_chunks[m][a],
+                    z_chunks[a][:, h * PIECE : (h + 1) * PIECE],
+                    start=(a == 0),
+                    stop=(a == CHUNKS - 1 and m < 2),
+                )
+
         for a in range(CHUNKS):
-            for m in range(3):
-                for h in range(HALVES):
-                    nc.tensor.matmul(
-                        sums[m][h][:],
-                        w_chunks[m][a],
-                        z_chunks[a][:, h * PIECE : (h + 1) * PIECE],
-                        start=(a == 0),
-                        stop=(a == CHUNKS - 1 and m < 2),
-                    )
+            project(0, a)
+            project(1, a)
+            if a >= LAG:
+                project(2, a - LAG)
 
         tables = [held.tile([P, S], BF16, name=f"table{m}") for m in range(2)]
         for m in range(2):
             nc.vector.tensor_copy(tables[m][:, 0:PIECE], sums[m][0][:])
             nc.scalar.copy(tables[m][:, PIECE:S], sums[m][1][:])
+
+        for a in range(CHUNKS - LAG, CHUNKS):
+            project(2, a)
 
         for h in range(HALVES):
             for m in range(2):

@@ -32,7 +32,8 @@ def tile_gnn_layer_b_kernel(tc, z, wsv, wsr, wdr, offs, out):
         for g, size in enumerate(LOADS):
             chunks = slice(len(z_chunks), len(z_chunks) + size)
             z_load = held.tile([P, size, S], BF16, name=f"z{g}")
-            nc.sync.dma_start(z_load[:], z_rows[:, chunks, :])
+            for columns in (slice(0, PIECE), slice(PIECE, S)) if g == 0 else (slice(0, S),):
+                nc.sync.dma_start(z_load[:, :, columns], z_rows[:, chunks, columns])
             z_chunks.extend(z_load[:, i, :] for i in range(size))
             for m in range(3):
                 w_load = held.tile([P, size, P], BF16, name=f"w{m}_{g}")
@@ -49,21 +50,21 @@ def tile_gnn_layer_b_kernel(tc, z, wsv, wsr, wdr, offs, out):
 
         sums = [[psum.tile([P, PIECE], F32, name=f"sum{m}_{h}") for h in range(HALVES)] for m in range(3)]
 
-        def project(m, a):
+        def project(ms, a):
             for h in range(HALVES):
-                nc.tensor.matmul(
-                    sums[m][h][:],
-                    w_chunks[m][a],
-                    z_chunks[a][:, h * PIECE : (h + 1) * PIECE],
-                    start=(a == 0),
-                    stop=(a == CHUNKS - 1 and m < 2),
-                )
+                for m in ms:
+                    nc.tensor.matmul(
+                        sums[m][h][:],
+                        w_chunks[m][a],
+                        z_chunks[a][:, h * PIECE : (h + 1) * PIECE],
+                        start=(a == 0),
+                        stop=(a == CHUNKS - 1 and m < 2),
+                    )
 
         for a in range(CHUNKS):
-            project(0, a)
-            project(1, a)
+            project((0, 1), a)
             if a >= LAG:
-                project(2, a - LAG)
+                project((2,), a - LAG)
 
         tables = [held.tile([P, S], BF16, name=f"table{m}") for m in range(2)]
         for m in range(2):
@@ -71,7 +72,7 @@ def tile_gnn_layer_b_kernel(tc, z, wsv, wsr, wdr, offs, out):
             nc.scalar.copy(tables[m][:, PIECE:S], sums[m][1][:])
 
         for a in range(CHUNKS - LAG, CHUNKS):
-            project(2, a)
+            project((2,), a)
 
         for h in range(HALVES):
             for m in range(2):

@@ -14,6 +14,9 @@ CHUNKS = F // P
 LOADS = (1, 1) + (2,) * 15
 assert sum(LOADS) == CHUNKS
 
+FIRST_PIECES = ((0, 128), (128, 384), (512, 512))
+OTHER_PIECES = ((0, PIECE), (PIECE, PIECE))
+
 LAG = 2
 
 FLOPS = 3 * 2 * F * P * S
@@ -32,8 +35,8 @@ def tile_gnn_layer_b_kernel(tc, z, wsv, wsr, wdr, offs, out):
         for g, size in enumerate(LOADS):
             chunks = slice(len(z_chunks), len(z_chunks) + size)
             z_load = held.tile([P, size, S], BF16, name=f"z{g}")
-            for columns in (slice(0, PIECE), slice(PIECE, S)) if g == 0 else (slice(0, S),):
-                nc.sync.dma_start(z_load[:, :, columns], z_rows[:, chunks, columns])
+            for first, width in FIRST_PIECES if g == 0 else ((0, S),):
+                nc.sync.dma_start(z_load[:, :, first : first + width], z_rows[:, chunks, first : first + width])
             z_chunks.extend(z_load[:, i, :] for i in range(size))
             for m in range(3):
                 w_load = held.tile([P, size, P], BF16, name=f"w{m}_{g}")
@@ -51,13 +54,14 @@ def tile_gnn_layer_b_kernel(tc, z, wsv, wsr, wdr, offs, out):
         sums = [[psum.tile([P, PIECE], F32, name=f"sum{m}_{h}") for h in range(HALVES)] for m in range(3)]
 
         def project(ms, a):
-            for h in range(HALVES):
+            for first, width in FIRST_PIECES if a == 0 else OTHER_PIECES:
+                h, column = divmod(first, PIECE)
                 for m in ms:
                     nc.tensor.matmul(
-                        sums[m][h][:],
+                        sums[m][h][:, column : column + width],
                         w_chunks[m][a],
-                        z_chunks[a][:, h * PIECE : (h + 1) * PIECE],
-                        start=(a == 0),
+                        z_chunks[a][:, first : first + width],
+                        start=(a == 0 and column == 0),
                         stop=(a == CHUNKS - 1 and m < 2),
                     )
 

@@ -11,8 +11,9 @@ N = 2 * SLOTS * S
 PIECE = 512
 HALVES = S // PIECE
 CHUNKS = F // P
-LOADS = (1, 1) + (2,) * 15
-assert sum(LOADS) == CHUNKS
+Z_LOADS = (1, 1) + (2,) * 15
+W_LOADS = (2, 2, 4, 8, 16)
+assert sum(Z_LOADS) == sum(W_LOADS) == CHUNKS
 
 FIRST_PIECES = ((0, 128), (128, 384), (512, 512))
 OTHER_PIECES = ((0, PIECE), (PIECE, PIECE))
@@ -32,12 +33,14 @@ def tile_gnn_layer_b_kernel(tc, z, wsv, wsr, wdr, offs, out):
         tc.psum_pool(name="psum", bufs=1) as psum,
     ):
         z_chunks, w_chunks = [], [[], [], []]
-        for g, size in enumerate(LOADS):
+        for g, size in enumerate(Z_LOADS):
             chunks = slice(len(z_chunks), len(z_chunks) + size)
             z_load = held.tile([P, size, S], BF16, name=f"z{g}")
             for first, width in FIRST_PIECES if g == 0 else ((0, S),):
                 nc.sync.dma_start(z_load[:, :, first : first + width], z_rows[:, chunks, first : first + width])
             z_chunks.extend(z_load[:, i, :] for i in range(size))
+        for g, size in enumerate(W_LOADS):
+            chunks = slice(len(w_chunks[0]), len(w_chunks[0]) + size)
             for m in range(3):
                 w_load = held.tile([P, size, P], BF16, name=f"w{m}_{g}")
                 nc.scalar.dma_start(w_load[:], w_rows[m][:, chunks, :])

@@ -92,6 +92,9 @@ def tile_gnn_layer_b_kernel(tc, z, wsv, wsr, wdr, offs, out):
                         start=False,
                         stop=(m == 1 and k == SLOTS - 1),
                     )
-            result = held.tile([P, PIECE], F32, name=f"result{h}")
-            nc.vector.tensor_relu(result[:], sums[2][h][:])
-            nc.sync.dma_start(out[:, h * PIECE : (h + 1) * PIECE], result[:])
+            queues = (nc.sync,) if h < HALVES - 1 else (nc.scalar, nc.sync)
+            width = PIECE // len(queues)
+            for step, queue in enumerate(queues):
+                result = held.tile([P, width], F32, name=f"result{h}_{step}")
+                nc.vector.tensor_relu(result[:], sums[2][h][:, step * width : (step + 1) * width])
+                queue.dma_start(out[:, h * PIECE + step * width : h * PIECE + (step + 1) * width], result[:])

@@ -18,6 +18,10 @@ assert sum(Z_LOADS) == sum(W_LOADS) == CHUNKS
 FIRST_PIECES = ((0, 128), (128, 384), (512, 512))
 OTHER_PIECES = ((0, PIECE), (PIECE, PIECE))
 
+PARTS = ((0, 512), (512, 384), (896, 128))
+EARLY_PARTS = (0, 1)
+LAST_PART = 2
+
 LAG = 2
 
 FLOPS = 3 * 2 * F * P * S
@@ -54,47 +58,71 @@ def tile_gnn_layer_b_kernel(tc, z, wsv, wsr, wdr, offs, out):
         quarter = held.tile([P, P], BF16, name="quarter")
         nc.vector.tensor_scalar_mul(quarter[:], identity[:], 1.0 / SLOTS)
 
-        sums = [[psum.tile([P, PIECE], F32, name=f"sum{m}_{h}") for h in range(HALVES)] for m in range(3)]
+        table_sums = [[psum.tile([P, PIECE], F32, name=f"table_sum{m}_{h}") for h in range(HALVES)] for m in range(2)]
+        node_sums = [psum.tile([P, PARTS[i][1]], F32, name=f"node_sum{i}") for i in EARLY_PARTS]
+        neighbour_sums = [psum.tile([P, PIECE], F32, name=f"neighbour_sum{h}") for h in range(HALVES)]
 
-        def project(ms, a):
+        def project_tables(a):
             for first, width in FIRST_PIECES if a == 0 else OTHER_PIECES:
                 h, column = divmod(first, PIECE)
-                for m in ms:
+                for m in range(2):
                     nc.tensor.matmul(
-                        sums[m][h][:, column : column + width],
+                        table_sums[m][h][:, column : column + width],
                         w_chunks[m][a],
                         z_chunks[a][:, first : first + width],
                         start=(a == 0 and column == 0),
-                        stop=(a == CHUNKS - 1 and m < 2),
+                        stop=(a == CHUNKS - 1),
                     )
 
+        def project_node(i, a):
+            first, width = PARTS[i]
+            nc.tensor.matmul(
+                node_sums[i][:], w_chunks[2][a], z_chunks[a][:, first : first + width], start=(a == 0), stop=(a == CHUNKS - 1)
+            )
+
         for a in range(CHUNKS):
-            project((0, 1), a)
+            project_tables(a)
             if a >= LAG:
-                project((2,), a - LAG)
+                for i in EARLY_PARTS:
+                    project_node(i, a - LAG)
 
         tables = [held.tile([P, S], BF16, name=f"table{m}") for m in range(2)]
         for m in range(2):
-            nc.vector.tensor_copy(tables[m][:, 0:PIECE], sums[m][0][:])
-            nc.scalar.copy(tables[m][:, PIECE:S], sums[m][1][:])
+            nc.vector.tensor_copy(tables[m][:, 0:PIECE], table_sums[m][0][:])
+            nc.scalar.copy(tables[m][:, PIECE:S], table_sums[m][1][:])
 
         for a in range(CHUNKS - LAG, CHUNKS):
-            project((2,), a)
+            for i in EARLY_PARTS:
+                project_node(i, a)
 
-        for h in range(HALVES):
+        neighbours = held.tile([P, S], F32, name="neighbours")
+
+        def look_up(h):
             for m in range(2):
                 for k in range(SLOTS):
                     first = (m * SLOTS * S + k * S + h * PIECE) // 16
                     nc.tensor.matmul(
-                        sums[2][h][:],
+                        neighbour_sums[h][:],
                         quarter[:],
                         tables[m][:].indirect(offsets[:, first : first + PIECE // 16]),
-                        start=False,
+                        start=(m == 0 and k == 0),
                         stop=(m == 1 and k == SLOTS - 1),
                     )
-            queues = (nc.sync,) if h < HALVES - 1 else (nc.scalar, nc.sync)
-            width = PIECE // len(queues)
-            for step, queue in enumerate(queues):
-                result = held.tile([P, width], F32, name=f"result{h}_{step}")
-                nc.vector.tensor_relu(result[:], sums[2][h][:, step * width : (step + 1) * width])
-                queue.dma_start(out[:, h * PIECE + step * width : h * PIECE + (step + 1) * width], result[:])
+            nc.scalar.copy(neighbours[:, h * PIECE : (h + 1) * PIECE], neighbour_sums[h][:])
+
+        def finish(i, queue):
+            first, width = PARTS[i]
+            total = held.tile([P, width], F32, name=f"total{i}")
+            nc.vector.tensor_add(total[:], node_sums[i][:], neighbours[:, first : first + width])
+            result = held.tile([P, width], F32, name=f"result{i}")
+            nc.vector.tensor_relu(result[:], total[:])
+            queue.dma_start(out[:, first : first + width], result[:])
+
+        look_up(0)
+        finish(0, nc.sync)
+        look_up(1)
+        finish(1, nc.scalar)
+        node_sums.append(psum.tile([P, PARTS[LAST_PART][1]], F32, name=f"node_sum{LAST_PART}", tag="neighbour_sum0"))
+        for a in range(CHUNKS):
+            project_node(LAST_PART, a)
+        finish(LAST_PART, nc.sync)

@@ -37,18 +37,33 @@ def tile_gnn_layer_b_kernel(tc, z, wsv, wsr, wdr, offs, out):
         tc.psum_pool(name="psum", bufs=1) as psum,
     ):
         z_chunks, w_chunks = [], [[], [], []]
-        for g, size in enumerate(Z_LOADS):
+        z_loads, w_loads = [], [[], [], []]
+
+        def load_z():
+            size = Z_LOADS[len(z_loads)]
             chunks = slice(len(z_chunks), len(z_chunks) + size)
-            z_load = held.tile([P, size, S], BF16, name=f"z{g}")
-            for first, width in FIRST_PIECES if g == 0 else ((0, S),):
+            z_load = held.tile([P, size, S], BF16, name=f"z{chunks.start}")
+            for first, width in FIRST_PIECES if chunks.start == 0 else ((0, S),):
                 nc.sync.dma_start(z_load[:, :, first : first + width], z_rows[:, chunks, first : first + width])
+            z_loads.append(z_load)
             z_chunks.extend(z_load[:, i, :] for i in range(size))
-        for g, size in enumerate(W_LOADS):
-            chunks = slice(len(w_chunks[0]), len(w_chunks[0]) + size)
-            for m in range(3):
-                w_load = held.tile([P, size, P], BF16, name=f"w{m}_{g}")
-                nc.scalar.dma_start(w_load[:], w_rows[m][:, chunks, :])
-                w_chunks[m].extend(w_load[:, i, :] for i in range(size))
+
+        def load_w(m):
+            size = W_LOADS[len(w_loads[m])]
+            chunks = slice(len(w_chunks[m]), len(w_chunks[m]) + size)
+            w_load = held.tile([P, size, P], BF16, name=f"w{m}_{chunks.start}")
+            nc.sync.dma_start(w_load[:], w_rows[m][:, chunks, :])
+            w_loads[m].append(w_load)
+            w_chunks[m].extend(w_load[:, i, :] for i in range(size))
+
+        for a in range(CHUNKS):
+            for m in range(2):
+                if a == len(w_chunks[m]):
+                    load_w(m)
+            if a == len(z_chunks):
+                load_z()
+            if a == len(w_chunks[2]):
+                load_w(2)
 
         offsets = held.tile([P, N // 16], U16, name="offsets")
         nc.sync.dma_start(offsets[:], offs)

@@ -11,8 +11,8 @@ N = 2 * SLOTS * S
 PIECE = 512
 HALVES = S // PIECE
 CHUNKS = F // P
-Z_LOADS = (1, 1) + (2,) * 15
-W_LOADS = (2, 2, 4, 8, 16)
+Z_LOADS = (1, 1, 1, 1) + (2,) * 14
+W_LOADS = (1, 3, 4, 8, 16)
 assert sum(Z_LOADS) == sum(W_LOADS) == CHUNKS
 
 FIRST_PIECES = ((0, 128), (128, 384), (512, 512))
@@ -62,7 +62,7 @@ def tile_gnn_layer_b_kernel(tc, z, wsv, wsr, wdr, offs, out):
                     load_w(m)
             if a == len(z_chunks):
                 load_z()
-            if a == len(w_chunks[2]):
+            if a - (LAG - 1) == len(w_chunks[2]):
                 load_w(2)
 
         offsets = held.tile([P, N // 16], U16, name="offsets")

@@ -22,7 +22,7 @@ PARTS = ((0, 512), (512, 384), (896, 128))
 EARLY_PARTS = (0, 1)
 LAST_PART = 2
 
-LAG = 2
+LAG = 3
 
 FLOPS = 3 * 2 * F * P * S
 
@@ -103,8 +103,8 @@ def tile_gnn_layer_b_kernel(tc, z, wsv, wsr, wdr, offs, out):
 
         tables = [held.tile([P, S], BF16, name=f"table{m}") for m in range(2)]
         for m in range(2):
-            nc.vector.tensor_copy(tables[m][:, 0:PIECE], table_sums[m][0][:])
-            nc.scalar.copy(tables[m][:, PIECE:S], table_sums[m][1][:])
+            for h in range(HALVES):
+                nc.vector.tensor_copy(tables[m][:, h * PIECE : (h + 1) * PIECE], table_sums[m][h][:])
 
         for a in range(CHUNKS - LAG, CHUNKS):
             for i in EARLY_PARTS:
@@ -123,7 +123,7 @@ def tile_gnn_layer_b_kernel(tc, z, wsv, wsr, wdr, offs, out):
                         start=(m == 0 and k == 0),
                         stop=(m == 1 and k == SLOTS - 1),
                     )
-            nc.scalar.copy(neighbours[:, h * PIECE : (h + 1) * PIECE], neighbour_sums[h][:])
+            nc.vector.tensor_copy(neighbours[:, h * PIECE : (h + 1) * PIECE], neighbour_sums[h][:])
 
         def finish(i, queue):
             first, width = PARTS[i]

@@ -39,14 +39,16 @@ def tile_gnn_layer_b_kernel(tc, z, wsv, wsr, wdr, offs, out):
         z_chunks, w_chunks = [], [[], [], []]
         z_loads, w_loads = [], [[], [], []]
 
-        def load_z():
+        def open_z():
             size = Z_LOADS[len(z_loads)]
             chunks = slice(len(z_chunks), len(z_chunks) + size)
             z_load = held.tile([P, size, S], BF16, name=f"z{chunks.start}")
-            for first, width in FIRST_PIECES if chunks.start == 0 else ((0, S),):
-                nc.sync.dma_start(z_load[:, :, first : first + width], z_rows[:, chunks, first : first + width])
             z_loads.append(z_load)
             z_chunks.extend(z_load[:, i, :] for i in range(size))
+            return [
+                (z_load[:, :, first : first + width], z_rows[:, chunks, first : first + width])
+                for first, width in (FIRST_PIECES if chunks.start == 0 else ((0, S),))
+            ]
 
         def load_w(m):
             size = W_LOADS[len(w_loads[m])]
@@ -57,11 +59,15 @@ def tile_gnn_layer_b_kernel(tc, z, wsv, wsr, wdr, offs, out):
             w_chunks[m].extend(w_load[:, i, :] for i in range(size))
 
         for a in range(CHUNKS):
-            for m in range(2):
-                if a == len(w_chunks[m]):
-                    load_w(m)
-            if a == len(z_chunks):
-                load_z()
+            pieces = open_z() if a == len(z_chunks) else []
+            if a == len(w_chunks[0]):
+                load_w(0)
+            for tile_part, z_part in pieces[:1]:
+                nc.sync.dma_start(tile_part, z_part)
+            if a == len(w_chunks[1]):
+                load_w(1)
+            for tile_part, z_part in pieces[1:]:
+                nc.sync.dma_start(tile_part, z_part)
             if a - (LAG - 1) == len(w_chunks[2]):
                 load_w(2)
 

@@ -19,10 +19,9 @@ FIRST_PIECES = ((0, 128), (128, 384), (512, 512))
 OTHER_PIECES = ((0, PIECE), (PIECE, PIECE))
 
 PARTS = ((0, 512), (512, 384), (896, 128))
-EARLY_PARTS = (0, 1)
 LAST_PART = 2
 
-LAG = 3
+LAG = 8
 
 FLOPS = 3 * 2 * F * P * S
 
@@ -80,8 +79,7 @@ def tile_gnn_layer_b_kernel(tc, z, wsv, wsr, wdr, offs, out):
         nc.vector.tensor_scalar_mul(quarter[:], identity[:], 1.0 / SLOTS)
 
         table_sums = [[psum.tile([P, PIECE], F32, name=f"table_sum{m}_{h}") for h in range(HALVES)] for m in range(2)]
-        node_sums = [psum.tile([P, PARTS[i][1]], F32, name=f"node_sum{i}") for i in EARLY_PARTS]
-        neighbour_sums = [psum.tile([P, PIECE], F32, name=f"neighbour_sum{h}") for h in range(HALVES)]
+        half_sums = [psum.tile([P, PIECE], F32, name=f"half_sum{h}") for h in range(HALVES)]
 
         def project_tables(a):
             for first, width in FIRST_PIECES if a == 0 else OTHER_PIECES:
@@ -95,17 +93,32 @@ def tile_gnn_layer_b_kernel(tc, z, wsv, wsr, wdr, offs, out):
                         stop=(a == CHUNKS - 1),
                     )
 
-        def project_node(i, a):
+        def project_node(i, a, sums, start, stop):
             first, width = PARTS[i]
-            nc.tensor.matmul(
-                node_sums[i][:], w_chunks[2][a], z_chunks[a][:, first : first + width], start=(a == 0), stop=(a == CHUNKS - 1)
-            )
+            nc.tensor.matmul(sums, w_chunks[2][a], z_chunks[a][:, first : first + width], start=start, stop=stop)
+
+        def look_up(h, start, stop):
+            for m in range(2):
+                for k in range(SLOTS):
+                    first = (m * SLOTS * S + k * S + h * PIECE) // 16
+                    nc.tensor.matmul(
+                        half_sums[h][:],
+                        quarter[:],
+                        tables[m][:].indirect(offsets[:, first : first + PIECE // 16]),
+                        start=(start and m == 0 and k == 0),
+                        stop=(stop and m == 1 and k == SLOTS - 1),
+                    )
+
+        def rectify_and_store(i, total, queue):
+            first, width = PARTS[i]
+            result = held.tile([P, width], F32, name=f"result{i}")
+            nc.vector.tensor_relu(result[:], total)
+            queue.dma_start(out[:, first : first + width], result[:])
 
         for a in range(CHUNKS):
             project_tables(a)
             if a >= LAG:
-                for i in EARLY_PARTS:
-                    project_node(i, a - LAG)
+                project_node(0, a - LAG, half_sums[0][:], start=(a == LAG), stop=False)
 
         tables = [held.tile([P, S], BF16, name=f"table{m}") for m in range(2)]
         for m in range(2):
@@ -113,37 +126,20 @@ def tile_gnn_layer_b_kernel(tc, z, wsv, wsr, wdr, offs, out):
                 nc.vector.tensor_copy(tables[m][:, h * PIECE : (h + 1) * PIECE], table_sums[m][h][:])
 
         for a in range(CHUNKS - LAG, CHUNKS):
-            for i in EARLY_PARTS:
-                project_node(i, a)
+            project_node(0, a, half_sums[0][:], start=False, stop=False)
 
-        neighbours = held.tile([P, S], F32, name="neighbours")
-
-        def look_up(h):
-            for m in range(2):
-                for k in range(SLOTS):
-                    first = (m * SLOTS * S + k * S + h * PIECE) // 16
-                    nc.tensor.matmul(
-                        neighbour_sums[h][:],
-                        quarter[:],
-                        tables[m][:].indirect(offsets[:, first : first + PIECE // 16]),
-                        start=(m == 0 and k == 0),
-                        stop=(m == 1 and k == SLOTS - 1),
-                    )
-            nc.vector.tensor_copy(neighbours[:, h * PIECE : (h + 1) * PIECE], neighbour_sums[h][:])
-
-        def finish(i, queue):
-            first, width = PARTS[i]
-            total = held.tile([P, width], F32, name=f"total{i}")
-            nc.vector.tensor_add(total[:], node_sums[i][:], neighbours[:, first : first + width])
-            result = held.tile([P, width], F32, name=f"result{i}")
-            nc.vector.tensor_relu(result[:], total[:])
-            queue.dma_start(out[:, first : first + width], result[:])
-
-        look_up(0)
-        finish(0, nc.sync)
-        look_up(1)
-        finish(1, nc.scalar)
-        node_sums.append(psum.tile([P, PARTS[LAST_PART][1]], F32, name=f"node_sum{LAST_PART}", tag="neighbour_sum0"))
+        look_up(0, start=False, stop=True)
+        rectify_and_store(0, half_sums[0][:], nc.sync)
+        look_up(1, start=True, stop=False)
         for a in range(CHUNKS):
-            project_node(LAST_PART, a)
-        finish(LAST_PART, nc.sync)
+            project_node(1, a, half_sums[1][:, : PARTS[1][1]], start=False, stop=(a == CHUNKS - 1))
+        last_width = PARTS[LAST_PART][1]
+        last_neighbours = held.tile([P, last_width], F32, name="last_neighbours")
+        nc.vector.tensor_copy(last_neighbours[:], half_sums[1][:, PARTS[1][1] :])
+        rectify_and_store(1, half_sums[1][:, : PARTS[1][1]], nc.scalar)
+        last_node = psum.tile([P, last_width], F32, name="last_node", tag="half_sum0")
+        for a in range(CHUNKS):
+            project_node(LAST_PART, a, last_node[:], start=(a == 0), stop=(a == CHUNKS - 1))
+        last_total = held.tile([P, last_width], F32, name="last_total")
+        nc.vector.tensor_add(last_total[:], last_node[:], last_neighbours[:])
+        rectify_and_store(LAST_PART, last_total[:], nc.sync)

@@ -79,7 +79,7 @@ def tile_gnn_layer_b_kernel(tc, z, wsv, wsr, wdr, offs, out):
         nc.vector.tensor_scalar_mul(quarter[:], identity[:], 1.0 / SLOTS)
 
         table_sums = [[psum.tile([P, PIECE], F32, name=f"table_sum{m}_{h}") for h in range(HALVES)] for m in range(2)]
-        half_sums = [psum.tile([P, PIECE], F32, name=f"half_sum{h}") for h in range(HALVES)]
+        part_sums = [psum.tile([P, width], F32, name=f"part_sum{i}") for i, (first, width) in enumerate(PARTS[:LAST_PART])]
 
         def project_tables(a):
             for first, width in FIRST_PIECES if a == 0 else OTHER_PIECES:
@@ -93,32 +93,33 @@ def tile_gnn_layer_b_kernel(tc, z, wsv, wsr, wdr, offs, out):
                         stop=(a == CHUNKS - 1),
                     )
 
-        def project_node(i, a, sums, start, stop):
+        def project_node(i, a, start, stop):
             first, width = PARTS[i]
-            nc.tensor.matmul(sums, w_chunks[2][a], z_chunks[a][:, first : first + width], start=start, stop=stop)
+            nc.tensor.matmul(part_sums[i][:], w_chunks[2][a], z_chunks[a][:, first : first + width], start=start, stop=stop)
 
-        def look_up(h, start, stop):
+        def look_up(i, start, stop):
+            first, width = PARTS[i]
             for m in range(2):
                 for k in range(SLOTS):
-                    first = (m * SLOTS * S + k * S + h * PIECE) // 16
+                    entry = (m * SLOTS * S + k * S + first) // 16
                     nc.tensor.matmul(
-                        half_sums[h][:],
+                        part_sums[i][:],
                         quarter[:],
-                        tables[m][:].indirect(offsets[:, first : first + PIECE // 16]),
+                        tables[m][:].indirect(offsets[:, entry : entry + width // 16]),
                         start=(start and m == 0 and k == 0),
                         stop=(stop and m == 1 and k == SLOTS - 1),
                     )
 
-        def rectify_and_store(i, total, queue):
+        def rectify_and_store(i, queue):
             first, width = PARTS[i]
             result = held.tile([P, width], F32, name=f"result{i}")
-            nc.vector.tensor_relu(result[:], total)
+            nc.vector.tensor_relu(result[:], part_sums[i][:])
             queue.dma_start(out[:, first : first + width], result[:])
 
         for a in range(CHUNKS):
             project_tables(a)
             if a >= LAG:
-                project_node(0, a - LAG, half_sums[0][:], start=(a == LAG), stop=False)
+                project_node(0, a - LAG, start=(a == LAG), stop=False)
 
         tables = [held.tile([P, S], BF16, name=f"table{m}") for m in range(2)]
         for m in range(2):
@@ -126,20 +127,16 @@ def tile_gnn_layer_b_kernel(tc, z, wsv, wsr, wdr, offs, out):
                 nc.vector.tensor_copy(tables[m][:, h * PIECE : (h + 1) * PIECE], table_sums[m][h][:])
 
         for a in range(CHUNKS - LAG, CHUNKS):
-            project_node(0, a, half_sums[0][:], start=False, stop=False)
+            project_node(0, a, start=False, stop=False)
 
         look_up(0, start=False, stop=True)
-        rectify_and_store(0, half_sums[0][:], nc.sync)
+        rectify_and_store(0, nc.sync)
         look_up(1, start=True, stop=False)
         for a in range(CHUNKS):
-            project_node(1, a, half_sums[1][:, : PARTS[1][1]], start=False, stop=(a == CHUNKS - 1))
-        last_width = PARTS[LAST_PART][1]
-        last_neighbours = held.tile([P, last_width], F32, name="last_neighbours")
-        nc.vector.tensor_copy(last_neighbours[:], half_sums[1][:, PARTS[1][1] :])
-        rectify_and_store(1, half_sums[1][:, : PARTS[1][1]], nc.scalar)
-        last_node = psum.tile([P, last_width], F32, name="last_node", tag="half_sum0")
+            project_node(1, a, start=False, stop=(a == CHUNKS - 1))
+        rectify_and_store(1, nc.scalar)
+        part_sums.append(psum.tile([P, PARTS[LAST_PART][1]], F32, name=f"part_sum{LAST_PART}", tag="part_sum0"))
+        look_up(LAST_PART, start=True, stop=False)
         for a in range(CHUNKS):
-            project_node(LAST_PART, a, last_node[:], start=(a == 0), stop=(a == CHUNKS - 1))
-        last_total = held.tile([P, last_width], F32, name="last_total")
-        nc.vector.tensor_add(last_total[:], last_node[:], last_neighbours[:])
-        rectify_and_store(LAST_PART, last_total[:], nc.sync)
+            project_node(LAST_PART, a, start=False, stop=(a == CHUNKS - 1))
+        rectify_and_store(LAST_PART, nc.sync)

@@ -11,11 +11,11 @@ N = 2 * SLOTS * S
 PIECE = 512
 HALVES = S // PIECE
 CHUNKS = F // P
-Z_LOADS = (1, 1, 1, 1) + (2,) * 14
-W_LOADS = (1, 3, 4, 8, 16)
+Z_LOADS = (1,) * 8 + (2,) * 12
+W_LOADS = (1, 1, 2, 4, 8, 16)
 assert sum(Z_LOADS) == sum(W_LOADS) == CHUNKS
 
-FIRST_PIECES = ((0, 128), (128, 384), (512, 512))
+FIRST_PIECES = ((0, 128), (128, 128), (256, 256), (512, 512))
 OTHER_PIECES = ((0, PIECE), (PIECE, PIECE))
 
 PARTS = ((0, 512), (512, 384), (896, 128))

import concourse.mybir as mybir
from concourse.masks import make_identity

BF16, F32, U16 = mybir.dt.bfloat16, mybir.dt.float32, mybir.dt.uint16

P = 128
F = 4096
S = 1024
SLOTS = 4
N = 2 * SLOTS * S
PIECE = 512
HALVES = S // PIECE
CHUNKS = F // P
Z_LOADS = (1,) * 8 + (2,) * 12
W_LOADS = (1, 1, 2, 4, 8, 16)
assert sum(Z_LOADS) == sum(W_LOADS) == CHUNKS

FIRST_PIECES = ((0, 128), (128, 128), (256, 256), (512, 512))
OTHER_PIECES = ((0, PIECE), (PIECE, PIECE))

PARTS = ((0, 512), (512, 384), (896, 128))
LAST_PART = 2

LAG = 8

FLOPS = 3 * 2 * F * P * S


def tile_gnn_layer_b_kernel(tc, z, wsv, wsr, wdr, offs, out):
    nc = tc.nc
    z_rows = z.rearrange("(p a) s -> p a s", p=P)
    w_rows = [w.rearrange("(p a) c -> p a c", p=P) for w in (wsr, wdr, wsv)]

    with (
        tc.tile_pool(name="held", bufs=1) as held,
        tc.psum_pool(name="psum", bufs=1) as psum,
    ):
        z_chunks, w_chunks = [], [[], [], []]
        z_loads, w_loads = [], [[], [], []]

        def open_z():
            size = Z_LOADS[len(z_loads)]
            chunks = slice(len(z_chunks), len(z_chunks) + size)
            z_load = held.tile([P, size, S], BF16, name=f"z{chunks.start}")
            z_loads.append(z_load)
            z_chunks.extend(z_load[:, i, :] for i in range(size))
            return [
                (z_load[:, :, first : first + width], z_rows[:, chunks, first : first + width])
                for first, width in (FIRST_PIECES if chunks.start == 0 else ((0, S),))
            ]

        def load_w(m):
            size = W_LOADS[len(w_loads[m])]
            chunks = slice(len(w_chunks[m]), len(w_chunks[m]) + size)
            w_load = held.tile([P, size, P], BF16, name=f"w{m}_{chunks.start}")
            nc.sync.dma_start(w_load[:], w_rows[m][:, chunks, :])
            w_loads[m].append(w_load)
            w_chunks[m].extend(w_load[:, i, :] for i in range(size))

        for a in range(CHUNKS):
            pieces = open_z() if a == len(z_chunks) else []
            if a == len(w_chunks[0]):
                load_w(0)
            for tile_part, z_part in pieces[:1]:
                nc.sync.dma_start(tile_part, z_part)
            if a == len(w_chunks[1]):
                load_w(1)
            for tile_part, z_part in pieces[1:]:
                nc.sync.dma_start(tile_part, z_part)
            if a - (LAG - 1) == len(w_chunks[2]):
                load_w(2)

        offsets = held.tile([P, N // 16], U16, name="offsets")
        nc.sync.dma_start(offsets[:], offs)

        identity = held.tile([P, P], BF16, name="identity")
        make_identity(nc, identity[:])
        quarter = held.tile([P, P], BF16, name="quarter")
        nc.vector.tensor_scalar_mul(quarter[:], identity[:], 1.0 / SLOTS)

        table_sums = [[psum.tile([P, PIECE], F32, name=f"table_sum{m}_{h}") for h in range(HALVES)] for m in range(2)]
        part_sums = [psum.tile([P, width], F32, name=f"part_sum{i}") for i, (first, width) in enumerate(PARTS[:LAST_PART])]

        def project_tables(a):
            for first, width in FIRST_PIECES if a == 0 else OTHER_PIECES:
                h, column = divmod(first, PIECE)
                for m in range(2):
                    nc.tensor.matmul(
                        table_sums[m][h][:, column : column + width],
                        w_chunks[m][a],
                        z_chunks[a][:, first : first + width],
                        start=(a == 0 and column == 0),
                        stop=(a == CHUNKS - 1),
                    )

        def project_node(i, a, start, stop):
            first, width = PARTS[i]
            nc.tensor.matmul(part_sums[i][:], w_chunks[2][a], z_chunks[a][:, first : first + width], start=start, stop=stop)

        def look_up(i, start, stop):
            first, width = PARTS[i]
            for m in range(2):
                for k in range(SLOTS):
                    entry = (m * SLOTS * S + k * S + first) // 16
                    nc.tensor.matmul(
                        part_sums[i][:],
                        quarter[:],
                        tables[m][:].indirect(offsets[:, entry : entry + width // 16]),
                        start=(start and m == 0 and k == 0),
                        stop=(stop and m == 1 and k == SLOTS - 1),
                    )

        def rectify_and_store(i, queue):
            first, width = PARTS[i]
            result = held.tile([P, width], F32, name=f"result{i}")
            nc.vector.tensor_relu(result[:], part_sums[i][:])
            queue.dma_start(out[:, first : first + width], result[:])

        for a in range(CHUNKS):
            project_tables(a)
            if a >= LAG:
                project_node(0, a - LAG, start=(a == LAG), stop=False)

        tables = [held.tile([P, S], BF16, name=f"table{m}") for m in range(2)]
        for m in range(2):
            for h in range(HALVES):
                nc.vector.tensor_copy(tables[m][:, h * PIECE : (h + 1) * PIECE], table_sums[m][h][:])

        for a in range(CHUNKS - LAG, CHUNKS):
            project_node(0, a, start=False, stop=False)

        look_up(0, start=False, stop=True)
        rectify_and_store(0, nc.sync)
        look_up(1, start=True, stop=False)
        for a in range(CHUNKS):
            project_node(1, a, start=False, stop=(a == CHUNKS - 1))
        rectify_and_store(1, nc.scalar)
        part_sums.append(psum.tile([P, PARTS[LAST_PART][1]], F32, name=f"part_sum{LAST_PART}", tag="part_sum0"))
        look_up(LAST_PART, start=True, stop=False)
        for a in range(CHUNKS):
            project_node(LAST_PART, a, start=False, stop=(a == CHUNKS - 1))
        rectify_and_store(LAST_PART, nc.sync)
